import numpy as np
import ml_dtypes


def mxq(x, axis, fmt="e4m3"):
    dtype, down = {"e4m3": (ml_dtypes.float8_e4m3fn, 7), "e5m2": (ml_dtypes.float8_e5m2, 14)}[fmt]
    v = np.moveaxis(np.asarray(x, np.float32).astype(ml_dtypes.bfloat16).astype(np.float64), axis, -1)
    blocks = v.reshape(v.shape[:-1] + (-1, 32))
    amax = np.abs(blocks).max(-1, keepdims=True)
    byte = np.maximum(np.where(amax > 0, np.frexp(amax)[1] - 1 + 127, 0) - down, 1)
    scale = np.exp2(byte - 127.0)
    codes = (blocks / scale).astype(np.float32).astype(dtype).astype(np.float64)
    return np.moveaxis((codes * scale).reshape(v.shape), -1, axis)


WIDE = False


def mx_kscale(k):
    if not WIDE:
        return np.ones(k)
    levels = np.array([10, -10, 5, -5, 0])
    a = np.random.permutation(np.resize(levels, k // 512 * 4)).reshape(k // 512, 4)
    idx = np.arange(k)
    return np.exp2(a[idx // 512, idx % 128 // 32])


BF16 = ml_dtypes.bfloat16


def bf(x):
    return np.asarray(x, np.float32).astype(BF16)


def f64(x):
    return np.asarray(x).astype(np.float64)


E2M1 = np.array([0.0, 0.5, 1.0, 1.5, 2.0, 3.0, 4.0, 6.0, -0.0, -0.5, -1.0, -1.5, -2.0, -3.0, -4.0, -6.0])


def pack_weight(w, fmt):
    k, n = w.shape
    w = f64(bf(w)).reshape(k // 32, 32, n)
    amax = np.abs(w).max(1)
    if fmt == "e4m3":
        byte = np.frexp(amax)[1] - 1 + 127 - 7
    else:
        mant, ex = np.frexp(amax / 6.0)
        byte = np.where(mant > 0.5, ex, ex - 1) + 127
    byte = np.clip(np.where(amax > 0, byte, 1), 1, 254)
    scaled = (w * np.exp2(127.0 - byte)[:, None, :]).reshape(k, n).astype(np.float32)
    by_word = np.ascontiguousarray(scaled.reshape(k // 512, 128, 4, n).transpose(0, 1, 3, 2))
    if fmt == "e4m3":
        words = by_word.astype(ml_dtypes.float8_e4m3fn).view(np.uint8)
    else:
        c = by_word.astype(ml_dtypes.float4_e2m1fn).view(np.uint8) & 0xF
        words = c[..., 0::2] | (c[..., 1::2] << 4)
    return np.ascontiguousarray(words), np.ascontiguousarray(byte.astype(np.uint8).reshape(k // 512, 16, n))


def unpack_weight(words, scales, fmt):
    g, p, n, _ = words.shape
    if fmt == "e4m3":
        vals = np.ascontiguousarray(words).view(ml_dtypes.float8_e4m3fn).astype(np.float64)
    else:
        nib = np.empty((g, p, n, 4), np.uint8)
        nib[..., 0::2] = words & 0xF
        nib[..., 1::2] = words >> 4
        vals = E2M1[nib]
    vals = vals * np.repeat(np.exp2(scales.astype(np.float64) - 127.0), 8, axis=1)[..., None]
    return vals.transpose(0, 1, 3, 2).reshape(g * 512, n)

def pack4(w):
    words, scales = pack_weight(w, "e2m1")
    return words.reshape(words.shape[0], 128, -1), scales


def unpack4(words, scales):
    return unpack_weight(words.reshape(words.shape[0], 128, -1, 2), scales, "e2m1")


B, Q, S, D = 16, 256, 512, 512
K = D + D


def sigmoid(v):
    return 1.0 / (1.0 + np.exp(-v))


def setup_inputs():
    t = mx_kscale(D)
    s = np.concatenate([np.ones(D), t])
    query = bf(np.random.standard_normal((B, Q, D)) * 0.25)
    weighted_ctx = bf(np.random.standard_normal((B, Q, D)) * 0.12 * t)
    W_lin_words, W_lin_scales = pack4(np.random.standard_normal((K, D)) * 5.0 / np.sqrt(K) / s[:, None])
    b_lin = bf(np.random.standard_normal(D) * 0.3)
    W_gate_words, W_gate_scales = pack4(np.random.standard_normal((K, D)) * 5.0 / np.sqrt(K) / s[:, None])
    b_gate = bf(np.random.standard_normal(D) * 0.3)
    return {"query": query,
            "weighted_ctx": weighted_ctx,
            "W_lin_words": W_lin_words,
            "W_lin_scales": W_lin_scales,
            "b_lin": b_lin,
            "W_gate_words": W_gate_words,
            "W_gate_scales": W_gate_scales,
            "b_gate": b_gate}


def reference(query, weighted_ctx, W_lin_words, W_lin_scales, b_lin, W_gate_words, W_gate_scales, b_gate):
    q = f64(query)
    cat = mxq(np.concatenate([q, f64(weighted_ctx)], axis=2), 2, "e4m3")
    h = np.tanh((cat @ unpack4(W_lin_words, W_lin_scales)) + f64(b_lin))
    g = sigmoid((cat @ unpack4(W_gate_words, W_gate_scales)) + f64(b_gate))
    return q * g + h * (1.0 - g)

@@ -1,0 +1,221 @@
+from contextlib import ExitStack
+
+import concourse.mybir as mybir
+from concourse.masks import make_identity
+
+F32 = mybir.dt.float32
+BF16 = mybir.dt.bfloat16
+I32 = mybir.dt.int32
+U32 = mybir.dt.uint32
+U8 = mybir.dt.uint8
+FP8X4 = mybir.dt.float8_e4m3fn_x4
+FP4X4 = mybir.dt.float4_e2m1fn_x4
+ALU = mybir.AluOpType
+ACT = mybir.ActivationFunctionType
+
+P = 128
+PACK = 4
+PAIR = 2
+TOKENS = 16 * 256
+D = 512
+PASSES = 2
+N_TILES = TOKENS // P
+GROUP_TILES = 4
+GROUP_TOKENS = GROUP_TILES * P
+CHUNKS = D // P
+STEP_TILES = 2
+STEPS_PER_GROUP = GROUP_TILES // STEP_TILES
+N_STEPS = N_TILES // STEP_TILES
+LEAD = 2
+LAG = 2
+SCALE_ROWS = 4
+
+FLOPS = 2 * TOKENS * (PASSES * D) * (2 * D)
+
+
+def tile_smcmr_pb_t_kernel(
+    tc, query, weighted_ctx, W_lin_words, W_lin_scales, b_lin, W_gate_words, W_gate_scales, b_gate, out
+):
+    nc = tc.nc
+    q_dram = query.flatten_outer_dims().rearrange("(p t) d -> p t d", t=N_TILES)
+    c_dram = weighted_ctx.flatten_outer_dims().rearrange("(p t) d -> p t d", t=N_TILES)
+    out_dram = out.flatten_outer_dims().rearrange("(p t) d -> p t d", t=N_TILES)
+
+    with ExitStack() as ctx:
+        ctx.enter_context(tc.manual_schedule())
+        const = ctx.enter_context(tc.tile_pool(name="const", bufs=1))
+        quant = ctx.enter_context(tc.tile_pool(name="quant", bufs=2))
+        h_pool = ctx.enter_context(tc.tile_pool(name="h_pool", bufs=3))
+        gate_pool = ctx.enter_context(tc.tile_pool(name="gate_pool", bufs=STEP_TILES * (LAG + 1)))
+        work = ctx.enter_context(tc.tile_pool(name="work", bufs=2 * STEP_TILES))
+        results = ctx.enter_context(tc.tile_pool(name="results", bufs=3))
+        flip_psum = ctx.enter_context(tc.psum_pool(name="flip_psum", bufs=2))
+        acc_psum = ctx.enter_context(tc.psum_pool(name="acc_psum", bufs=3))
+        back_psum = ctx.enter_context(tc.psum_pool(name="back_psum", bufs=3))
+
+        q_all = const.tile([P, N_TILES, D], BF16)
+        c_all = const.tile([P, N_TILES, D], BF16)
+
+        def load_step(step):
+            tiles = slice(step * STEP_TILES, (step + 1) * STEP_TILES)
+            nc.sync.dma_start(out=q_all[:, tiles, :], in_=q_dram[:, tiles, :])
+            nc.sync.dma_start(out=c_all[:, tiles, :], in_=c_dram[:, tiles, :])
+
+        def load_weight(words_dram, scales_dram, words, planes):
+            for quadrant in range(P // 32):
+                rows = slice(SCALE_ROWS * quadrant, SCALE_ROWS * (quadrant + 1))
+                nc.sync.dma_start(
+                    out=planes[32 * quadrant : 32 * quadrant + SCALE_ROWS, :, :].bitcast(I32),
+                    in_=scales_dram[:, rows, :].rearrange("g r n -> r g n").bitcast(I32),
+                )
+            nc.sync.dma_start(out=words[:].bitcast(I32), in_=words_dram.rearrange("g p b -> p g b").bitcast(I32))
+
+        lin_words = const.tile([P, PASSES, 2 * D], U8, align_bytes=64)
+        lin_planes = const.tile([P, PASSES, D], U8, align_bytes=64)
+        gate_words = const.tile([P, PASSES, 2 * D], U8, align_bytes=64)
+        gate_planes = const.tile([P, PASSES, D], U8, align_bytes=64)
+        nc.vector.memset(lin_planes[:].bitcast(I32), 0)
+        nc.vector.memset(gate_planes[:].bitcast(I32), 0)
+
+        load_step(0)
+        load_weight(W_lin_words, W_lin_scales, lin_words, lin_planes)
+        load_weight(W_gate_words, W_gate_scales, gate_words, gate_planes)
+        for step in range(1, N_STEPS):
+            load_step(step)
+
+        ident = const.tile([P, P], F32)
+        make_identity(nc, ident[:])
+
+        gate_bias = const.tile([P, D], BF16)
+        nc.scalar.dma_start(out=gate_bias[:], in_=b_gate.partition_broadcast(P))
+
+        lin_bias_rows = const.tile([P, P], BF16)
+        nc.vector.memset(lin_bias_rows[:], 0.0)
+        nc.scalar.dma_start(out=lin_bias_rows[0:CHUNKS, :], in_=b_lin.rearrange("(j m) -> j m", m=P))
+        lin_bias_rows_f32 = const.tile([P, P], F32)
+        nc.vector.tensor_copy(out=lin_bias_rows_f32[:], in_=lin_bias_rows[:])
+        lin_bias_flipped = flip_psum.tile([P, P], F32, tag="flipped")
+        nc.tensor.transpose(lin_bias_flipped[:], lin_bias_rows_f32[:], ident[:])
+        lin_bias = const.tile([P, CHUNKS], F32)
+        nc.vector.tensor_copy(out=lin_bias[:], in_=lin_bias_flipped[:, 0:CHUNKS])
+
+        warm = const.tile([P, 1], F32)
+        nc.vector.memset(warm[:], 0.0)
+        nc.scalar.activation(out=warm[:], in_=warm[:], func=ACT.Sigmoid)
+
+        grouped_of = {}
+        codes_of = {}
+        h_t_of = {}
+        gate_of = {}
+        blend_of = {}
+
+        def transpose_cat(step):
+            group, part = divmod(step, STEPS_PER_GROUP)
+            if part == 0:
+                grouped = quant.tile([P, PASSES, GROUP_TOKENS, PACK], BF16, align_bytes=64)
+                grouped_of[group] = grouped
+            grouped_words = grouped_of[group][:].bitcast(F32)
+            for i in range(STEP_TILES):
+                tile_index = step * STEP_TILES + i
+                first = (part * STEP_TILES + i) * P
+                flipped = flip_psum.tile([P, PASSES, PAIR, P], F32, tag="flipped")
+                for g, resident in enumerate((q_all, c_all)):
+                    words = resident[:, tile_index, :].bitcast(F32)
+                    for u in range(PAIR):
+                        nc.tensor.transpose(flipped[:, g, u, :], words[:, u : D // PAIR : PAIR], ident[:])
+                nc.scalar.copy(
+                    out=grouped_words[:, :, first : first + P, :],
+                    in_=flipped[:].rearrange("p g u r -> p g r u"),
+                )
+
+        def quantise_cat(step):
+            group, part = divmod(step, STEPS_PER_GROUP)
+            if part == 0:
+                codes = quant.tile([P, PASSES, GROUP_TOKENS], U32, align_bytes=64)
+                planes = quant.tile([P, PASSES, GROUP_TOKENS], U8, align_bytes=64)
+                codes_of[group] = (codes, planes)
+            codes, planes = codes_of[group]
+            tokens = slice(part * STEP_TILES * P, (part + 1) * STEP_TILES * P)
+            for g in range(PASSES):
+                nc.vector.quantize_mx(
+                    out=codes[:, g, tokens].bitcast(FP8X4),
+                    scales=planes[:, g, tokens],
+                    in_=grouped_of[group][:, g, tokens, :].rearrange("p r t -> p (r t)"),
+                )
+
+        def matmuls(step):
+            group, part = divmod(step, STEPS_PER_GROUP)
+            codes, planes = codes_of[group]
+            if part == 0:
+                h_t = h_pool.tile([P, CHUNKS, GROUP_TOKENS], F32)
+                h_t_of[group] = h_t
+            h_t = h_t_of[group]
+            for i in range(STEP_TILES):
+                j = part * STEP_TILES + i
+                lin_acc = acc_psum.tile([P, GROUP_TOKENS], F32, tag="acc")
+                for g in range(PASSES):
+                    nc.tensor.matmul_mx(
+                        out=lin_acc[:],
+                        lhsT=lin_words[:, g, 2 * j * P : 2 * (j + 1) * P].bitcast(FP4X4),
+                        lhsT_scale=lin_planes[:, g, j * P : (j + 1) * P],
+                        rhs=codes[:, g, :].bitcast(FP8X4),
+                        rhs_scale=planes[:, g, :],
+                        start=(g == 0),
+                        stop=(g == PASSES - 1),
+                    )
+                nc.scalar.activation(
+                    out=h_t[:, j, :], in_=lin_acc[:], func=ACT.Tanh, bias=lin_bias[:, j : j + 1], scale=1.0
+                )
+                gate_acc = acc_psum.tile([P, D], F32, tag="acc")
+                for g in range(PASSES):
+                    nc.tensor.matmul_mx(
+                        out=gate_acc[:],
+                        lhsT=codes[:, g, j * P : (j + 1) * P].bitcast(FP8X4),
+                        lhsT_scale=planes[:, g, j * P : (j + 1) * P],
+                        rhs=gate_words[:, g, :].bitcast(FP4X4),
+                        rhs_scale=gate_planes[:, g, :],
+                        start=(g == 0),
+                        stop=(g == PASSES - 1),
+                    )
+                gate = gate_pool.tile([P, D], F32)
+                nc.vector.tensor_tensor(out=gate[:], in0=gate_acc[:], in1=gate_bias[:], op=ALU.add)
+                gate_of[step * STEP_TILES + i] = gate
+            for i in range(STEP_TILES):
+                gate = gate_of[step * STEP_TILES + i]
+                nc.scalar.activation(out=gate[:], in_=gate[:], func=ACT.Sigmoid)
+
+        def blend_front(step):
+            group, part = divmod(step, STEPS_PER_GROUP)
+            h_t = h_t_of[group]
+            for i in range(STEP_TILES):
+                tile_index = step * STEP_TILES + i
+                first = (part * STEP_TILES + i) * P
+                h_bank = back_psum.tile([P, D], F32)
+                for j in range(CHUNKS):
+                    nc.tensor.transpose(h_bank[:, j * P : (j + 1) * P], h_t[:, j, first : first + P], ident[:])
+                diff = work.tile([P, D], F32)
+                nc.vector.tensor_tensor(out=diff[:], in0=q_all[:, tile_index, :], in1=h_bank[:], op=ALU.subtract)
+                gated = work.tile([P, D], F32)
+                nc.gpsimd.tensor_tensor(out=gated[:], in0=gate_of[tile_index][:], in1=diff[:], op=ALU.mult)
+                blend_of[tile_index] = (h_bank, gated)
+
+        def blend_back(step):
+            tiles = slice(step * STEP_TILES, (step + 1) * STEP_TILES)
+            result = results.tile([P, STEP_TILES, D], F32)
+            for i in range(STEP_TILES):
+                h_bank, gated = blend_of[step * STEP_TILES + i]
+                nc.vector.tensor_tensor(out=result[:, i, :], in0=gated[:], in1=h_bank[:], op=ALU.add)
+            nc.sync.dma_start(out=out_dram[:, tiles, :], in_=result[:])
+
+        for step in range(-LEAD, N_STEPS + LAG):
+            ahead, behind = step + LEAD, step - LAG
+            if ahead < N_STEPS:
+                transpose_cat(ahead)
+            if 0 <= behind:
+                blend_front(behind)
+            if ahead < N_STEPS:
+                quantise_cat(ahead)
+            if 0 <= step < N_STEPS:
+                matmuls(step)
+            if 0 <= behind:
+                blend_back(behind)

@@ -23,11 +23,12 @@ N_TILES = TOKENS // P
 GROUP_TILES = 4
 GROUP_TOKENS = GROUP_TILES * P
 CHUNKS = D // P
-STEP_TILES = 2
+STEP_TILES = 1
+LOAD_TILES = 2
 STEPS_PER_GROUP = GROUP_TILES // STEP_TILES
 N_STEPS = N_TILES // STEP_TILES
-LEAD = 2
-LAG = 2
+LEAD = STEPS_PER_GROUP
+LAG = STEPS_PER_GROUP
 SCALE_ROWS = 4
 
 FLOPS = 2 * TOKENS * (PASSES * D) * (2 * D)
@@ -47,7 +48,7 @@ def tile_smcmr_pb_t_kernel(
         quant = ctx.enter_context(tc.tile_pool(name="quant", bufs=2))
         h_pool = ctx.enter_context(tc.tile_pool(name="h_pool", bufs=3))
         gate_pool = ctx.enter_context(tc.tile_pool(name="gate_pool", bufs=STEP_TILES * (LAG + 1)))
-        work = ctx.enter_context(tc.tile_pool(name="work", bufs=2 * STEP_TILES))
+        work = ctx.enter_context(tc.tile_pool(name="work", bufs=4))
         results = ctx.enter_context(tc.tile_pool(name="results", bufs=3))
         flip_psum = ctx.enter_context(tc.psum_pool(name="flip_psum", bufs=2))
         acc_psum = ctx.enter_context(tc.psum_pool(name="acc_psum", bufs=3))
@@ -56,8 +57,8 @@ def tile_smcmr_pb_t_kernel(
         q_all = const.tile([P, N_TILES, D], BF16)
         c_all = const.tile([P, N_TILES, D], BF16)
 
-        def load_step(step):
-            tiles = slice(step * STEP_TILES, (step + 1) * STEP_TILES)
+        def load_tiles(first_tile):
+            tiles = slice(first_tile, first_tile + LOAD_TILES)
             nc.sync.dma_start(out=q_all[:, tiles, :], in_=q_dram[:, tiles, :])
             nc.sync.dma_start(out=c_all[:, tiles, :], in_=c_dram[:, tiles, :])
 
@@ -77,11 +78,11 @@ def tile_smcmr_pb_t_kernel(
         nc.vector.memset(lin_planes[:].bitcast(I32), 0)
         nc.vector.memset(gate_planes[:].bitcast(I32), 0)
 
-        load_step(0)
+        load_tiles(0)
         load_weight(W_lin_words, W_lin_scales, lin_words, lin_planes)
         load_weight(W_gate_words, W_gate_scales, gate_words, gate_planes)
-        for step in range(1, N_STEPS):
-            load_step(step)
+        for first_tile in range(LOAD_TILES, N_TILES, LOAD_TILES):
+            load_tiles(first_tile)
 
         ident = const.tile([P, P], F32)
         make_identity(nc, ident[:])

@@ -23,13 +23,15 @@ N_TILES = TOKENS // P
 GROUP_TILES = 4
 GROUP_TOKENS = GROUP_TILES * P
 CHUNKS = D // P
-STEP_TILES = 1
-LOAD_TILES = 2
+STEP_TILES = 2
 STEPS_PER_GROUP = GROUP_TILES // STEP_TILES
 N_STEPS = N_TILES // STEP_TILES
-LEAD = STEPS_PER_GROUP
-LAG = STEPS_PER_GROUP
 SCALE_ROWS = 4
+FLIP_LEAD = 3
+QUANT_LEAD = 2
+TANH_LAG = 1
+GATE_LAG = 2
+FINISH_LAG = 3
 
 FLOPS = 2 * TOKENS * (PASSES * D) * (2 * D)
 
@@ -46,30 +48,32 @@ def tile_smcmr_pb_t_kernel(
         ctx.enter_context(tc.manual_schedule())
         const = ctx.enter_context(tc.tile_pool(name="const", bufs=1))
         quant = ctx.enter_context(tc.tile_pool(name="quant", bufs=2))
-        h_pool = ctx.enter_context(tc.tile_pool(name="h_pool", bufs=3))
-        gate_pool = ctx.enter_context(tc.tile_pool(name="gate_pool", bufs=STEP_TILES * (LAG + 1)))
-        work = ctx.enter_context(tc.tile_pool(name="work", bufs=4))
+        g_pool = ctx.enter_context(tc.tile_pool(name="g_pool", bufs=3))
+        h_pool = ctx.enter_context(tc.tile_pool(name="h_pool", bufs=STEP_TILES * (FINISH_LAG + 1)))
+        work = ctx.enter_context(tc.tile_pool(name="work", bufs=3 * STEP_TILES))
         results = ctx.enter_context(tc.tile_pool(name="results", bufs=3))
-        flip_psum = ctx.enter_context(tc.psum_pool(name="flip_psum", bufs=2))
-        acc_psum = ctx.enter_context(tc.psum_pool(name="acc_psum", bufs=3))
-        back_psum = ctx.enter_context(tc.psum_pool(name="back_psum", bufs=3))
+        flip_psum = ctx.enter_context(tc.psum_pool(name="flip_psum", bufs=STEP_TILES))
+        acc_psum = ctx.enter_context(tc.psum_pool(name="acc_psum", bufs=2 * STEP_TILES))
+        back_psum = ctx.enter_context(tc.psum_pool(name="back_psum", bufs=STEP_TILES))
 
         q_all = const.tile([P, N_TILES, D], BF16)
         c_all = const.tile([P, N_TILES, D], BF16)
 
-        def load_tiles(first_tile):
-            tiles = slice(first_tile, first_tile + LOAD_TILES)
+        def load_step(step):
+            tiles = slice(step * STEP_TILES, (step + 1) * STEP_TILES)
             nc.sync.dma_start(out=q_all[:, tiles, :], in_=q_dram[:, tiles, :])
             nc.sync.dma_start(out=c_all[:, tiles, :], in_=c_dram[:, tiles, :])
 
-        def load_weight(words_dram, scales_dram, words, planes):
+        def load_words(words_dram, words):
+            nc.sync.dma_start(out=words[:].bitcast(I32), in_=words_dram.rearrange("g p b -> p g b").bitcast(I32))
+
+        def load_scales(scales_dram, planes):
             for quadrant in range(P // 32):
                 rows = slice(SCALE_ROWS * quadrant, SCALE_ROWS * (quadrant + 1))
                 nc.sync.dma_start(
                     out=planes[32 * quadrant : 32 * quadrant + SCALE_ROWS, :, :].bitcast(I32),
                     in_=scales_dram[:, rows, :].rearrange("g r n -> r g n").bitcast(I32),
                 )
-            nc.sync.dma_start(out=words[:].bitcast(I32), in_=words_dram.rearrange("g p b -> p g b").bitcast(I32))
 
         lin_words = const.tile([P, PASSES, 2 * D], U8, align_bytes=64)
         lin_planes = const.tile([P, PASSES, D], U8, align_bytes=64)
@@ -78,27 +82,32 @@ def tile_smcmr_pb_t_kernel(
         nc.vector.memset(lin_planes[:].bitcast(I32), 0)
         nc.vector.memset(gate_planes[:].bitcast(I32), 0)
 
-        load_tiles(0)
-        load_weight(W_lin_words, W_lin_scales, lin_words, lin_planes)
-        load_weight(W_gate_words, W_gate_scales, gate_words, gate_planes)
-        for first_tile in range(LOAD_TILES, N_TILES, LOAD_TILES):
-            load_tiles(first_tile)
+        for step in range(STEPS_PER_GROUP):
+            load_step(step)
+        load_words(W_gate_words, gate_words)
+        load_words(W_lin_words, lin_words)
+        load_scales(W_gate_scales, gate_planes)
+        load_scales(W_lin_scales, lin_planes)
+        for step in range(STEPS_PER_GROUP, N_STEPS):
+            load_step(step)
 
         ident = const.tile([P, P], F32)
         make_identity(nc, ident[:])
 
-        gate_bias = const.tile([P, D], BF16)
-        nc.scalar.dma_start(out=gate_bias[:], in_=b_gate.partition_broadcast(P))
+        lin_bias = const.tile([P, D], BF16)
+        nc.scalar.dma_start(out=lin_bias[:], in_=b_lin.partition_broadcast(P))
 
-        lin_bias_rows = const.tile([P, P], BF16)
-        nc.vector.memset(lin_bias_rows[:], 0.0)
-        nc.scalar.dma_start(out=lin_bias_rows[0:CHUNKS, :], in_=b_lin.rearrange("(j m) -> j m", m=P))
-        lin_bias_rows_f32 = const.tile([P, P], F32)
-        nc.vector.tensor_copy(out=lin_bias_rows_f32[:], in_=lin_bias_rows[:])
-        lin_bias_flipped = flip_psum.tile([P, P], F32, tag="flipped")
-        nc.tensor.transpose(lin_bias_flipped[:], lin_bias_rows_f32[:], ident[:])
-        lin_bias = const.tile([P, CHUNKS], F32)
-        nc.vector.tensor_copy(out=lin_bias[:], in_=lin_bias_flipped[:, 0:CHUNKS])
+        gate_bias_rows = const.tile([P, P], BF16)
+        nc.vector.memset(gate_bias_rows[:], 0.0)
+        nc.scalar.dma_start(out=gate_bias_rows[0:CHUNKS, :], in_=b_gate.rearrange("(j m) -> j m", m=P))
+        gate_bias_rows_f32 = const.tile([P, P], F32)
+        nc.vector.tensor_copy(out=gate_bias_rows_f32[:], in_=gate_bias_rows[:])
+        gate_bias = const.tile([P, CHUNKS], F32)
+
+        def transpose_gate_bias():
+            gate_bias_flipped = flip_psum.tile([P, P], F32, tag="flipped")
+            nc.tensor.transpose(gate_bias_flipped[:], gate_bias_rows_f32[:], ident[:])
+            nc.vector.tensor_copy(out=gate_bias[:], in_=gate_bias_flipped[:, 0:CHUNKS])
 
         warm = const.tile([P, 1], F32)
         nc.vector.memset(warm[:], 0.0)
@@ -106,9 +115,10 @@ def tile_smcmr_pb_t_kernel(
 
         grouped_of = {}
         codes_of = {}
-        h_t_of = {}
-        gate_of = {}
-        blend_of = {}
+        g_t_of = {}
+        h_of = {}
+        diff_of = {}
+        gated_of = {}
 
         def transpose_cat(step):
             group, part = divmod(step, STEPS_PER_GROUP)
@@ -148,75 +158,92 @@ def tile_smcmr_pb_t_kernel(
             group, part = divmod(step, STEPS_PER_GROUP)
             codes, planes = codes_of[group]
             if part == 0:
-                h_t = h_pool.tile([P, CHUNKS, GROUP_TOKENS], F32)
-                h_t_of[group] = h_t
-            h_t = h_t_of[group]
-            for i in range(STEP_TILES):
-                j = part * STEP_TILES + i
-                lin_acc = acc_psum.tile([P, GROUP_TOKENS], F32, tag="acc")
+                g_t = g_pool.tile([P, CHUNKS, GROUP_TOKENS], F32)
+                g_t_of[group] = g_t
+            for j in range(part * STEP_TILES, (part + 1) * STEP_TILES):
+                gate_acc = acc_psum.tile([P, GROUP_TOKENS], F32, tag="acc")
                 for g in range(PASSES):
                     nc.tensor.matmul_mx(
-                        out=lin_acc[:],
-                        lhsT=lin_words[:, g, 2 * j * P : 2 * (j + 1) * P].bitcast(FP4X4),
-                        lhsT_scale=lin_planes[:, g, j * P : (j + 1) * P],
+                        out=gate_acc[:],
+                        lhsT=gate_words[:, g, 2 * j * P : 2 * (j + 1) * P].bitcast(FP4X4),
+                        lhsT_scale=gate_planes[:, g, j * P : (j + 1) * P],
                         rhs=codes[:, g, :].bitcast(FP8X4),
                         rhs_scale=planes[:, g, :],
                         start=(g == 0),
                         stop=(g == PASSES - 1),
                     )
                 nc.scalar.activation(
-                    out=h_t[:, j, :], in_=lin_acc[:], func=ACT.Tanh, bias=lin_bias[:, j : j + 1], scale=1.0
+                    out=g_t_of[group][:, j, :],
+                    in_=gate_acc[:],
+                    func=ACT.Sigmoid,
+                    bias=gate_bias[:, j : j + 1],
+                    scale=1.0,
                 )
-                gate_acc = acc_psum.tile([P, D], F32, tag="acc")
+            for t in range(part * STEP_TILES, (part + 1) * STEP_TILES):
+                lin_acc = acc_psum.tile([P, D], F32, tag="acc")
                 for g in range(PASSES):
                     nc.tensor.matmul_mx(
-                        out=gate_acc[:],
-                        lhsT=codes[:, g, j * P : (j + 1) * P].bitcast(FP8X4),
-                        lhsT_scale=planes[:, g, j * P : (j + 1) * P],
-                        rhs=gate_words[:, g, :].bitcast(FP4X4),
-                        rhs_scale=gate_planes[:, g, :],
+                        out=lin_acc[:],
+                        lhsT=codes[:, g, t * P : (t + 1) * P].bitcast(FP8X4),
+                        lhsT_scale=planes[:, g, t * P : (t + 1) * P],
+                        rhs=lin_words[:, g, :].bitcast(FP4X4),
+                        rhs_scale=lin_planes[:, g, :],
                         start=(g == 0),
                         stop=(g == PASSES - 1),
                     )
-                gate = gate_pool.tile([P, D], F32)
-                nc.vector.tensor_tensor(out=gate[:], in0=gate_acc[:], in1=gate_bias[:], op=ALU.add)
-                gate_of[step * STEP_TILES + i] = gate
-            for i in range(STEP_TILES):
-                gate = gate_of[step * STEP_TILES + i]
-                nc.scalar.activation(out=gate[:], in_=gate[:], func=ACT.Sigmoid)
+                h = h_pool.tile([P, D], F32)
+                nc.vector.tensor_tensor(out=h[:], in0=lin_acc[:], in1=lin_bias[:], op=ALU.add)
+                h_of[group * GROUP_TILES + t] = h
 
-        def blend_front(step):
-            group, part = divmod(step, STEPS_PER_GROUP)
-            h_t = h_t_of[group]
-            for i in range(STEP_TILES):
-                tile_index = step * STEP_TILES + i
-                first = (part * STEP_TILES + i) * P
-                h_bank = back_psum.tile([P, D], F32)
-                for j in range(CHUNKS):
-                    nc.tensor.transpose(h_bank[:, j * P : (j + 1) * P], h_t[:, j, first : first + P], ident[:])
+        def tanh_and_difference(step):
+            for tile_index in range(step * STEP_TILES, (step + 1) * STEP_TILES):
+                h = h_of[tile_index]
+                nc.scalar.activation(out=h[:], in_=h[:], func=ACT.Tanh)
                 diff = work.tile([P, D], F32)
-                nc.vector.tensor_tensor(out=diff[:], in0=q_all[:, tile_index, :], in1=h_bank[:], op=ALU.subtract)
-                gated = work.tile([P, D], F32)
-                nc.gpsimd.tensor_tensor(out=gated[:], in0=gate_of[tile_index][:], in1=diff[:], op=ALU.mult)
-                blend_of[tile_index] = (h_bank, gated)
+                nc.gpsimd.tensor_tensor(out=diff[:], in0=q_all[:, tile_index, :], in1=h[:], op=ALU.subtract)
+                diff_of[tile_index] = diff
 
-        def blend_back(step):
-            tiles = slice(step * STEP_TILES, (step + 1) * STEP_TILES)
+        def apply_gate(step):
+            group, part = divmod(step, STEPS_PER_GROUP)
+            g_t = g_t_of[group]
+            for t in range(part * STEP_TILES, (part + 1) * STEP_TILES):
+                tile_index = group * GROUP_TILES + t
+                g_bank = back_psum.tile([P, D], F32)
+                for j in range(CHUNKS):
+                    nc.tensor.transpose(g_bank[:, j * P : (j + 1) * P], g_t[:, j, t * P : (t + 1) * P], ident[:])
+                gated = work.tile([P, D], F32)
+                nc.vector.tensor_tensor(out=gated[:], in0=diff_of[tile_index][:], in1=g_bank[:], op=ALU.mult)
+                gated_of[tile_index] = gated
+
+        def finish(step):
             result = results.tile([P, STEP_TILES, D], F32)
             for i in range(STEP_TILES):
-                h_bank, gated = blend_of[step * STEP_TILES + i]
-                nc.vector.tensor_tensor(out=result[:, i, :], in0=gated[:], in1=h_bank[:], op=ALU.add)
+                tile_index = step * STEP_TILES + i
+                nc.vector.tensor_tensor(
+                    out=result[:, i, :], in0=gated_of[tile_index][:], in1=h_of[tile_index][:], op=ALU.add
+                )
+            tiles = slice(step * STEP_TILES, (step + 1) * STEP_TILES)
             nc.sync.dma_start(out=out_dram[:, tiles, :], in_=result[:])
 
-        for step in range(-LEAD, N_STEPS + LAG):
-            ahead, behind = step + LEAD, step - LAG
-            if ahead < N_STEPS:
-                transpose_cat(ahead)
-            if 0 <= behind:
-                blend_front(behind)
-            if ahead < N_STEPS:
-                quantise_cat(ahead)
-            if 0 <= step < N_STEPS:
+        def exists(step):
+            return 0 <= step < N_STEPS
+
+        def one_round(step):
+            if exists(step + FLIP_LEAD):
+                transpose_cat(step + FLIP_LEAD)
+            if exists(step + QUANT_LEAD):
+                quantise_cat(step + QUANT_LEAD)
+            if exists(step - FINISH_LAG):
+                finish(step - FINISH_LAG)
+            if exists(step - GATE_LAG):
+                apply_gate(step - GATE_LAG)
+            if exists(step - TANH_LAG):
+                tanh_and_difference(step - TANH_LAG)
+            if exists(step):
                 matmuls(step)
-            if 0 <= behind:
-                blend_back(behind)
+
+        for step in range(-FLIP_LEAD, 0):
+            one_round(step)
+        transpose_gate_bias()
+        for step in range(0, N_STEPS + FINISH_LAG):
+            one_round(step)

@@ -20,18 +20,19 @@ TOKENS = 16 * 256
 D = 512
 PASSES = 2
 N_TILES = TOKENS // P
+CHUNKS = D // P
 GROUP_TILES = 4
 GROUP_TOKENS = GROUP_TILES * P
-CHUNKS = D // P
 STEP_TILES = 2
+STEP_TOKENS = STEP_TILES * P
 STEPS_PER_GROUP = GROUP_TILES // STEP_TILES
 N_STEPS = N_TILES // STEP_TILES
+FLIP_LEAD = 2
+QUANT_LEAD = 1
+GATE_LAG = 1
+BACK_LAG = 2
+BLEND_LAG = 3
 SCALE_ROWS = 4
-FLIP_LEAD = 3
-QUANT_LEAD = 2
-TANH_LAG = 1
-GATE_LAG = 2
-FINISH_LAG = 3
 
 FLOPS = 2 * TOKENS * (PASSES * D) * (2 * D)
 
@@ -47,14 +48,30 @@ def tile_smcmr_pb_t_kernel(
     with ExitStack() as ctx:
         ctx.enter_context(tc.manual_schedule())
         const = ctx.enter_context(tc.tile_pool(name="const", bufs=1))
-        quant = ctx.enter_context(tc.tile_pool(name="quant", bufs=2))
+        quant = ctx.enter_context(tc.tile_pool(name="quant", bufs=3))
         g_pool = ctx.enter_context(tc.tile_pool(name="g_pool", bufs=3))
-        h_pool = ctx.enter_context(tc.tile_pool(name="h_pool", bufs=STEP_TILES * (FINISH_LAG + 1)))
-        work = ctx.enter_context(tc.tile_pool(name="work", bufs=3 * STEP_TILES))
+        h_pool = ctx.enter_context(tc.tile_pool(name="h_pool", bufs=STEP_TILES * (BLEND_LAG + 2)))
+        work = ctx.enter_context(tc.tile_pool(name="work", bufs=4 * STEP_TILES))
         results = ctx.enter_context(tc.tile_pool(name="results", bufs=3))
         flip_psum = ctx.enter_context(tc.psum_pool(name="flip_psum", bufs=STEP_TILES))
-        acc_psum = ctx.enter_context(tc.psum_pool(name="acc_psum", bufs=2 * STEP_TILES))
+        lin_psum = ctx.enter_context(tc.psum_pool(name="lin_psum", bufs=STEP_TILES))
+        gate_psum = ctx.enter_context(tc.psum_pool(name="gate_psum", bufs=STEP_TILES))
         back_psum = ctx.enter_context(tc.psum_pool(name="back_psum", bufs=STEP_TILES))
+
+        warm = const.tile([P, 1], F32)
+        nc.vector.memset(warm[:], 0.0)
+        nc.scalar.activation(out=warm[:], in_=warm[:], func=ACT.Sigmoid)
+
+        lin_words = const.tile([P, PASSES, 2 * D], U8, align_bytes=64)
+        lin_planes = const.tile([P, PASSES, D], U8, align_bytes=64)
+        gate_words = const.tile([P, PASSES, 2 * D], U8, align_bytes=64)
+        gate_planes = const.tile([P, PASSES, D], U8, align_bytes=64)
+        nc.vector.memset(lin_planes[:].bitcast(I32), 0)
+        nc.vector.memset(gate_planes[:].bitcast(I32), 0)
+        gate_bias_rows = const.tile([P, P], BF16)
+        nc.vector.memset(gate_bias_rows[:], 0.0)
+        ident = const.tile([P, P], F32)
+        make_identity(nc, ident[:])
 
         q_all = const.tile([P, N_TILES, D], BF16)
         c_all = const.tile([P, N_TILES, D], BF16)
@@ -64,10 +81,8 @@ def tile_smcmr_pb_t_kernel(
             nc.sync.dma_start(out=q_all[:, tiles, :], in_=q_dram[:, tiles, :])
             nc.sync.dma_start(out=c_all[:, tiles, :], in_=c_dram[:, tiles, :])
 
-        def load_words(words_dram, words):
+        def load_weight(words_dram, words, scales_dram, planes):
             nc.sync.dma_start(out=words[:].bitcast(I32), in_=words_dram.rearrange("g p b -> p g b").bitcast(I32))
-
-        def load_scales(scales_dram, planes):
             for quadrant in range(P // 32):
                 rows = slice(SCALE_ROWS * quadrant, SCALE_ROWS * (quadrant + 1))
                 nc.sync.dma_start(
@@ -75,69 +90,55 @@ def tile_smcmr_pb_t_kernel(
                     in_=scales_dram[:, rows, :].rearrange("g r n -> r g n").bitcast(I32),
                 )
 
-        lin_words = const.tile([P, PASSES, 2 * D], U8, align_bytes=64)
-        lin_planes = const.tile([P, PASSES, D], U8, align_bytes=64)
-        gate_words = const.tile([P, PASSES, 2 * D], U8, align_bytes=64)
-        gate_planes = const.tile([P, PASSES, D], U8, align_bytes=64)
-        nc.vector.memset(lin_planes[:].bitcast(I32), 0)
-        nc.vector.memset(gate_planes[:].bitcast(I32), 0)
-
-        for step in range(STEPS_PER_GROUP):
-            load_step(step)
-        load_words(W_gate_words, gate_words)
-        load_words(W_lin_words, lin_words)
-        load_scales(W_gate_scales, gate_planes)
-        load_scales(W_lin_scales, lin_planes)
-        for step in range(STEPS_PER_GROUP, N_STEPS):
-            load_step(step)
-
-        ident = const.tile([P, P], F32)
-        make_identity(nc, ident[:])
-
+        load_step(0)
+        load_weight(W_lin_words, lin_words, W_lin_scales, lin_planes)
+        load_step(1)
+        load_weight(W_gate_words, gate_words, W_gate_scales, gate_planes)
+        nc.sync.dma_start(out=gate_bias_rows[0:CHUNKS, :], in_=b_gate.rearrange("(j m) -> j m", m=P))
         lin_bias = const.tile([P, D], BF16)
-        nc.scalar.dma_start(out=lin_bias[:], in_=b_lin.partition_broadcast(P))
+        nc.sync.dma_start(out=lin_bias[:], in_=b_lin.partition_broadcast(P))
+        for step in range(2, N_STEPS):
+            load_step(step)
 
-        gate_bias_rows = const.tile([P, P], BF16)
-        nc.vector.memset(gate_bias_rows[:], 0.0)
-        nc.scalar.dma_start(out=gate_bias_rows[0:CHUNKS, :], in_=b_gate.rearrange("(j m) -> j m", m=P))
         gate_bias_rows_f32 = const.tile([P, P], F32)
-        nc.vector.tensor_copy(out=gate_bias_rows_f32[:], in_=gate_bias_rows[:])
         gate_bias = const.tile([P, CHUNKS], F32)
 
         def transpose_gate_bias():
-            gate_bias_flipped = flip_psum.tile([P, P], F32, tag="flipped")
-            nc.tensor.transpose(gate_bias_flipped[:], gate_bias_rows_f32[:], ident[:])
-            nc.vector.tensor_copy(out=gate_bias[:], in_=gate_bias_flipped[:, 0:CHUNKS])
+            nc.vector.tensor_copy(out=gate_bias_rows_f32[:], in_=gate_bias_rows[:])
+            flipped = flip_psum.tile([P, P], F32, tag="flipped")
+            nc.tensor.transpose(flipped[:], gate_bias_rows_f32[:], ident[:])
+            nc.vector.tensor_copy(out=gate_bias[:], in_=flipped[:, 0:CHUNKS])
 
-        warm = const.tile([P, 1], F32)
-        nc.vector.memset(warm[:], 0.0)
-        nc.scalar.activation(out=warm[:], in_=warm[:], func=ACT.Sigmoid)
-
+        flipped_of = {}
         grouped_of = {}
         codes_of = {}
-        g_t_of = {}
+        lin_of = {}
         h_of = {}
-        diff_of = {}
-        gated_of = {}
+        gate_of = {}
+        g_t_of = {}
+        back_of = {}
+        query_g_of = {}
+        rest_of = {}
+        result_of = {}
 
-        def transpose_cat(step):
-            group, part = divmod(step, STEPS_PER_GROUP)
-            if part == 0:
+        def transpose_cat(tile_index):
+            flipped = flip_psum.tile([P, PASSES, PAIR, P], F32, tag="flipped")
+            for g, resident in enumerate((q_all, c_all)):
+                words = resident[:, tile_index, :].bitcast(F32)
+                for u in range(PAIR):
+                    nc.tensor.transpose(flipped[:, g, u, :], words[:, u : D // PAIR : PAIR], ident[:])
+            flipped_of[tile_index] = flipped
+
+        def copy_cat(tile_index, copy):
+            group, i = divmod(tile_index, GROUP_TILES)
+            if i == 0:
                 grouped = quant.tile([P, PASSES, GROUP_TOKENS, PACK], BF16, align_bytes=64)
                 grouped_of[group] = grouped
             grouped_words = grouped_of[group][:].bitcast(F32)
-            for i in range(STEP_TILES):
-                tile_index = step * STEP_TILES + i
-                first = (part * STEP_TILES + i) * P
-                flipped = flip_psum.tile([P, PASSES, PAIR, P], F32, tag="flipped")
-                for g, resident in enumerate((q_all, c_all)):
-                    words = resident[:, tile_index, :].bitcast(F32)
-                    for u in range(PAIR):
-                        nc.tensor.transpose(flipped[:, g, u, :], words[:, u : D // PAIR : PAIR], ident[:])
-                nc.scalar.copy(
-                    out=grouped_words[:, :, first : first + P, :],
-                    in_=flipped[:].rearrange("p g u r -> p g r u"),
-                )
+            copy(
+                out=grouped_words[:, :, i * P : (i + 1) * P, :],
+                in_=flipped_of[tile_index][:].rearrange("p g u r -> p g r u"),
+            )
 
         def quantise_cat(step):
             group, part = divmod(step, STEPS_PER_GROUP)
@@ -146,7 +147,7 @@ def tile_smcmr_pb_t_kernel(
                 planes = quant.tile([P, PASSES, GROUP_TOKENS], U8, align_bytes=64)
                 codes_of[group] = (codes, planes)
             codes, planes = codes_of[group]
-            tokens = slice(part * STEP_TILES * P, (part + 1) * STEP_TILES * P)
+            tokens = slice(part * STEP_TOKENS, (part + 1) * STEP_TOKENS)
             for g in range(PASSES):
                 nc.vector.quantize_mx(
                     out=codes[:, g, tokens].bitcast(FP8X4),
@@ -154,96 +155,142 @@ def tile_smcmr_pb_t_kernel(
                     in_=grouped_of[group][:, g, tokens, :].rearrange("p r t -> p (r t)"),
                 )
 
-        def matmuls(step):
-            group, part = divmod(step, STEPS_PER_GROUP)
+        def multiply_lin(tile_index):
+            group, i = divmod(tile_index, GROUP_TILES)
             codes, planes = codes_of[group]
-            if part == 0:
+            lin = lin_psum.tile([P, D], F32)
+            for g in range(PASSES):
+                nc.tensor.matmul_mx(
+                    out=lin[:],
+                    lhsT=codes[:, g, i * P : (i + 1) * P].bitcast(FP8X4),
+                    lhsT_scale=planes[:, g, i * P : (i + 1) * P],
+                    rhs=lin_words[:, g, :].bitcast(FP4X4),
+                    rhs_scale=lin_planes[:, g, :],
+                    start=(g == 0),
+                    stop=(g == PASSES - 1),
+                )
+            lin_of[tile_index] = lin
+
+        def add_lin_bias(tile_index):
+            h = h_pool.tile([P, D], F32)
+            nc.vector.tensor_tensor(out=h[:], in0=lin_of[tile_index][:], in1=lin_bias[:], op=ALU.add)
+            h_of[tile_index] = h
+
+        def tanh(tile_index):
+            h = h_of[tile_index]
+            nc.scalar.activation(out=h[:], in_=h[:], func=ACT.Tanh)
+
+        def multiply_gate(step, i):
+            group, part = divmod(step, STEPS_PER_GROUP)
+            j = part * STEP_TILES + i
+            codes, planes = codes_of[group]
+            gate = gate_psum.tile([P, GROUP_TOKENS], F32)
+            for g in range(PASSES):
+                nc.tensor.matmul_mx(
+                    out=gate[:],
+                    lhsT=gate_words[:, g, 2 * j * P : 2 * (j + 1) * P].bitcast(FP4X4),
+                    lhsT_scale=gate_planes[:, g, j * P : (j + 1) * P],
+                    rhs=codes[:, g, :].bitcast(FP8X4),
+                    rhs_scale=planes[:, g, :],
+                    start=(g == 0),
+                    stop=(g == PASSES - 1),
+                )
+            gate_of[step, i] = gate
+
+        def sigmoid(step, i):
+            group, part = divmod(step, STEPS_PER_GROUP)
+            j = part * STEP_TILES + i
+            if j == 0:
                 g_t = g_pool.tile([P, CHUNKS, GROUP_TOKENS], F32)
                 g_t_of[group] = g_t
-            for j in range(part * STEP_TILES, (part + 1) * STEP_TILES):
-                gate_acc = acc_psum.tile([P, GROUP_TOKENS], F32, tag="acc")
-                for g in range(PASSES):
-                    nc.tensor.matmul_mx(
-                        out=gate_acc[:],
-                        lhsT=gate_words[:, g, 2 * j * P : 2 * (j + 1) * P].bitcast(FP4X4),
-                        lhsT_scale=gate_planes[:, g, j * P : (j + 1) * P],
-                        rhs=codes[:, g, :].bitcast(FP8X4),
-                        rhs_scale=planes[:, g, :],
-                        start=(g == 0),
-                        stop=(g == PASSES - 1),
-                    )
-                nc.scalar.activation(
-                    out=g_t_of[group][:, j, :],
-                    in_=gate_acc[:],
-                    func=ACT.Sigmoid,
-                    bias=gate_bias[:, j : j + 1],
-                    scale=1.0,
+            nc.scalar.activation(
+                out=g_t_of[group][:, j, :],
+                in_=gate_of[step, i][:],
+                func=ACT.Sigmoid,
+                bias=gate_bias[:, j : j + 1],
+                scale=1.0,
+            )
+
+        def transpose_g(tile_index):
+            group, i = divmod(tile_index, GROUP_TILES)
+            back = back_psum.tile([P, D], F32)
+            for j in range(CHUNKS):
+                nc.tensor.transpose(
+                    back[:, j * P : (j + 1) * P], g_t_of[group][:, j, i * P : (i + 1) * P], ident[:]
                 )
-            for t in range(part * STEP_TILES, (part + 1) * STEP_TILES):
-                lin_acc = acc_psum.tile([P, D], F32, tag="acc")
-                for g in range(PASSES):
-                    nc.tensor.matmul_mx(
-                        out=lin_acc[:],
-                        lhsT=codes[:, g, t * P : (t + 1) * P].bitcast(FP8X4),
-                        lhsT_scale=planes[:, g, t * P : (t + 1) * P],
-                        rhs=lin_words[:, g, :].bitcast(FP4X4),
-                        rhs_scale=lin_planes[:, g, :],
-                        start=(g == 0),
-                        stop=(g == PASSES - 1),
-                    )
-                h = h_pool.tile([P, D], F32)
-                nc.vector.tensor_tensor(out=h[:], in0=lin_acc[:], in1=lin_bias[:], op=ALU.add)
-                h_of[group * GROUP_TILES + t] = h
+            back_of[tile_index] = back
 
-        def tanh_and_difference(step):
-            for tile_index in range(step * STEP_TILES, (step + 1) * STEP_TILES):
-                h = h_of[tile_index]
-                nc.scalar.activation(out=h[:], in_=h[:], func=ACT.Tanh)
-                diff = work.tile([P, D], F32)
-                nc.gpsimd.tensor_tensor(out=diff[:], in0=q_all[:, tile_index, :], in1=h[:], op=ALU.subtract)
-                diff_of[tile_index] = diff
+        def blend(tile_index):
+            query_g = work.tile([P, D], F32)
+            nc.vector.tensor_tensor(
+                out=query_g[:], in0=q_all[:, tile_index, :], in1=back_of[tile_index][:], op=ALU.mult
+            )
+            rest = work.tile([P, D], F32)
+            nc.vector.scalar_tensor_tensor(
+                out=rest[:],
+                in0=back_of[tile_index][:],
+                scalar=1.0,
+                in1=h_of[tile_index][:],
+                op0=ALU.subtract,
+                op1=ALU.mult,
+            )
+            query_g_of[tile_index] = query_g
+            rest_of[tile_index] = rest
 
-        def apply_gate(step):
-            group, part = divmod(step, STEPS_PER_GROUP)
-            g_t = g_t_of[group]
-            for t in range(part * STEP_TILES, (part + 1) * STEP_TILES):
-                tile_index = group * GROUP_TILES + t
-                g_bank = back_psum.tile([P, D], F32)
-                for j in range(CHUNKS):
-                    nc.tensor.transpose(g_bank[:, j * P : (j + 1) * P], g_t[:, j, t * P : (t + 1) * P], ident[:])
-                gated = work.tile([P, D], F32)
-                nc.vector.tensor_tensor(out=gated[:], in0=diff_of[tile_index][:], in1=g_bank[:], op=ALU.mult)
-                gated_of[tile_index] = gated
+        def finish(tile_index):
+            step, i = divmod(tile_index, STEP_TILES)
+            if i == 0:
+                result = results.tile([P, STEP_TILES, D], F32)
+                result_of[step] = result
+            result = result_of[step]
+            engine = nc.vector if tile_index == N_TILES - 1 else nc.gpsimd
+            engine.tensor_tensor(
+                out=result[:, i, :], in0=query_g_of[tile_index][:], in1=rest_of[tile_index][:], op=ALU.subtract
+            )
+            if step == N_STEPS - 1:
+                nc.sync.dma_start(out=out_dram[:, tile_index, :], in_=result[:, i, :])
+            elif i == STEP_TILES - 1:
+                tiles = slice(step * STEP_TILES, (step + 1) * STEP_TILES)
+                nc.sync.dma_start(out=out_dram[:, tiles, :], in_=result[:])
 
-        def finish(step):
-            result = results.tile([P, STEP_TILES, D], F32)
-            for i in range(STEP_TILES):
-                tile_index = step * STEP_TILES + i
-                nc.vector.tensor_tensor(
-                    out=result[:, i, :], in0=gated_of[tile_index][:], in1=h_of[tile_index][:], op=ALU.add
-                )
-            tiles = slice(step * STEP_TILES, (step + 1) * STEP_TILES)
-            nc.sync.dma_start(out=out_dram[:, tiles, :], in_=result[:])
+        def tiles_of(step):
+            return range(step * STEP_TILES, (step + 1) * STEP_TILES) if 0 <= step < N_STEPS else ()
 
         def exists(step):
             return 0 <= step < N_STEPS
 
         def one_round(step):
-            if exists(step + FLIP_LEAD):
-                transpose_cat(step + FLIP_LEAD)
+            lin_tiles = tiles_of(step)
+            gate_parts = [(step - GATE_LAG, i) for i in range(STEP_TILES)] if exists(step - GATE_LAG) else []
+            blend_tiles = tiles_of(step - BLEND_LAG)
+            for tile_index in lin_tiles:
+                multiply_lin(tile_index)
+            for part in gate_parts:
+                multiply_gate(*part)
+            for tile_index in blend_tiles[:1]:
+                blend(tile_index)
+            for tile_index in lin_tiles:
+                add_lin_bias(tile_index)
+            for tile_index in blend_tiles[1:]:
+                blend(tile_index)
+            for tile_index in lin_tiles[:1]:
+                tanh(tile_index)
+            for part in gate_parts:
+                sigmoid(*part)
+            for tile_index in lin_tiles[1:]:
+                tanh(tile_index)
+            for tile_index in tiles_of(step + FLIP_LEAD):
+                transpose_cat(tile_index)
+                copy_cat(tile_index, nc.vector.tensor_copy if tile_index == 1 else nc.scalar.copy)
             if exists(step + QUANT_LEAD):
                 quantise_cat(step + QUANT_LEAD)
-            if exists(step - FINISH_LAG):
-                finish(step - FINISH_LAG)
-            if exists(step - GATE_LAG):
-                apply_gate(step - GATE_LAG)
-            if exists(step - TANH_LAG):
-                tanh_and_difference(step - TANH_LAG)
-            if exists(step):
-                matmuls(step)
+            for tile_index in tiles_of(step - BACK_LAG):
+                transpose_g(tile_index)
+            for tile_index in blend_tiles:
+                finish(tile_index)
 
         for step in range(-FLIP_LEAD, 0):
             one_round(step)
         transpose_gate_bias()
-        for step in range(0, N_STEPS + FINISH_LAG):
+        for step in range(0, N_STEPS + BLEND_LAG):
             one_round(step)

@@ -130,11 +130,11 @@ def tile_smcmr_pb_t_kernel(
             flipped_of[tile_index] = flipped
 
         def copy_cat(tile_index, copy):
-            group, i = divmod(tile_index, GROUP_TILES)
+            step, i = divmod(tile_index, STEP_TILES)
             if i == 0:
-                grouped = quant.tile([P, PASSES, GROUP_TOKENS, PACK], BF16, align_bytes=64)
-                grouped_of[group] = grouped
-            grouped_words = grouped_of[group][:].bitcast(F32)
+                grouped = quant.tile([P, PASSES, STEP_TOKENS, PACK], BF16, align_bytes=64)
+                grouped_of[step] = grouped
+            grouped_words = grouped_of[step][:].bitcast(F32)
             copy(
                 out=grouped_words[:, :, i * P : (i + 1) * P, :],
                 in_=flipped_of[tile_index][:].rearrange("p g u r -> p g r u"),
@@ -152,7 +152,7 @@ def tile_smcmr_pb_t_kernel(
                 nc.vector.quantize_mx(
                     out=codes[:, g, tokens].bitcast(FP8X4),
                     scales=planes[:, g, tokens],
-                    in_=grouped_of[group][:, g, tokens, :].rearrange("p r t -> p (r t)"),
+                    in_=grouped_of[step][:, g, :, :].rearrange("p r t -> p (r t)"),
                 )
 
         def multiply_lin(tile_index):

@@ -30,8 +30,9 @@ N_STEPS = N_TILES // STEP_TILES
 FLIP_LEAD = 2
 QUANT_LEAD = 1
 GATE_LAG = 1
-BACK_LAG = 2
-BLEND_LAG = 3
+TANH_LAG = 1
+BACK_LAG = 3
+BLEND_LAG = 4
 SCALE_ROWS = 4
 
 FLOPS = 2 * TOKENS * (PASSES * D) * (2 * D)
@@ -262,31 +263,26 @@ def tile_smcmr_pb_t_kernel(
         def one_round(step):
             lin_tiles = tiles_of(step)
             gate_parts = [(step - GATE_LAG, i) for i in range(STEP_TILES)] if exists(step - GATE_LAG) else []
-            blend_tiles = tiles_of(step - BLEND_LAG)
             for tile_index in lin_tiles:
                 multiply_lin(tile_index)
             for part in gate_parts:
                 multiply_gate(*part)
-            for tile_index in blend_tiles[:1]:
+            for tile_index in tiles_of(step - BLEND_LAG):
                 blend(tile_index)
+            if exists(step + QUANT_LEAD):
+                quantise_cat(step + QUANT_LEAD)
             for tile_index in lin_tiles:
                 add_lin_bias(tile_index)
-            for tile_index in blend_tiles[1:]:
-                blend(tile_index)
-            for tile_index in lin_tiles[:1]:
+            for tile_index in tiles_of(step - TANH_LAG):
                 tanh(tile_index)
             for part in gate_parts:
                 sigmoid(*part)
-            for tile_index in lin_tiles[1:]:
-                tanh(tile_index)
+            for tile_index in tiles_of(step - BACK_LAG):
+                transpose_g(tile_index)
             for tile_index in tiles_of(step + FLIP_LEAD):
                 transpose_cat(tile_index)
                 copy_cat(tile_index, nc.vector.tensor_copy if tile_index == 1 else nc.scalar.copy)
-            if exists(step + QUANT_LEAD):
-                quantise_cat(step + QUANT_LEAD)
-            for tile_index in tiles_of(step - BACK_LAG):
-                transpose_g(tile_index)
-            for tile_index in blend_tiles:
+            for tile_index in tiles_of(step - BLEND_LAG):
                 finish(tile_index)
 
         for step in range(-FLIP_LEAD, 0):

@@ -31,8 +31,8 @@ FLIP_LEAD = 2
 QUANT_LEAD = 1
 GATE_LAG = 1
 TANH_LAG = 1
-BACK_LAG = 3
-BLEND_LAG = 4
+BACK_LAG = 2
+BLEND_LAG = 3
 SCALE_ROWS = 4
 
 FLOPS = 2 * TOKENS * (PASSES * D) * (2 * D)
@@ -261,28 +261,32 @@ def tile_smcmr_pb_t_kernel(
             return 0 <= step < N_STEPS
 
         def one_round(step):
-            lin_tiles = tiles_of(step)
             gate_parts = [(step - GATE_LAG, i) for i in range(STEP_TILES)] if exists(step - GATE_LAG) else []
-            for tile_index in lin_tiles:
-                multiply_lin(tile_index)
+            lin_tiles = tiles_of(step)
+            blend_tiles = tiles_of(step - BLEND_LAG)
             for part in gate_parts:
                 multiply_gate(*part)
-            for tile_index in tiles_of(step - BLEND_LAG):
+            for tile_index in lin_tiles:
+                multiply_lin(tile_index)
+            for tile_index in tiles_of(step + QUANT_LEAD):
+                copy_cat(tile_index, nc.vector.tensor_copy if tile_index == 1 else nc.scalar.copy)
+            for tile_index in blend_tiles[:1]:
                 blend(tile_index)
             if exists(step + QUANT_LEAD):
                 quantise_cat(step + QUANT_LEAD)
+            for tile_index in blend_tiles[1:]:
+                blend(tile_index)
             for tile_index in lin_tiles:
                 add_lin_bias(tile_index)
-            for tile_index in tiles_of(step - TANH_LAG):
-                tanh(tile_index)
             for part in gate_parts:
                 sigmoid(*part)
-            for tile_index in tiles_of(step - BACK_LAG):
-                transpose_g(tile_index)
+            for tile_index in tiles_of(step - TANH_LAG):
+                tanh(tile_index)
             for tile_index in tiles_of(step + FLIP_LEAD):
                 transpose_cat(tile_index)
-                copy_cat(tile_index, nc.vector.tensor_copy if tile_index == 1 else nc.scalar.copy)
-            for tile_index in tiles_of(step - BLEND_LAG):
+            for tile_index in tiles_of(step - BACK_LAG):
+                transpose_g(tile_index)
+            for tile_index in blend_tiles:
                 finish(tile_index)
 
         for step in range(-FLIP_LEAD, 0):

@@ -67,10 +67,14 @@ def tile_smcmr_pb_t_kernel(
         lin_planes = const.tile([P, PASSES, D], U8, align_bytes=64)
         gate_words = const.tile([P, PASSES, 2 * D], U8, align_bytes=64)
         gate_planes = const.tile([P, PASSES, D], U8, align_bytes=64)
-        nc.vector.memset(lin_planes[:].bitcast(I32), 0)
-        nc.vector.memset(gate_planes[:].bitcast(I32), 0)
         gate_bias_rows = const.tile([P, P], BF16)
         nc.vector.memset(gate_bias_rows[:], 0.0)
+        lin_bias_row = const.tile([P, D], BF16)
+        nc.vector.memset(lin_bias_row[:], 0.0)
+        ones = const.tile([P, P], BF16)
+        nc.vector.memset(ones[:], 1.0)
+        nc.vector.memset(lin_planes[:].bitcast(I32), 0)
+        nc.vector.memset(gate_planes[:].bitcast(I32), 0)
         ident = const.tile([P, P], F32)
         make_identity(nc, ident[:])
 
@@ -91,24 +95,25 @@ def tile_smcmr_pb_t_kernel(
                     in_=scales_dram[:, rows, :].rearrange("g r n -> r g n").bitcast(I32),
                 )
 
+        nc.sync.dma_start(out=gate_bias_rows[0:CHUNKS, :], in_=b_gate.rearrange("(j m) -> j m", m=P))
+        nc.sync.dma_start(out=lin_bias_row[0:1, :], in_=b_lin.rearrange("(o d) -> o d", o=1))
         load_step(0)
         load_weight(W_lin_words, lin_words, W_lin_scales, lin_planes)
         load_step(1)
         load_weight(W_gate_words, gate_words, W_gate_scales, gate_planes)
-        nc.sync.dma_start(out=gate_bias_rows[0:CHUNKS, :], in_=b_gate.rearrange("(j m) -> j m", m=P))
-        lin_bias = const.tile([P, D], BF16)
-        nc.sync.dma_start(out=lin_bias[:], in_=b_lin.partition_broadcast(P))
         for step in range(2, N_STEPS):
             load_step(step)
 
-        gate_bias_rows_f32 = const.tile([P, P], F32)
+        chosen_columns = const.tile([P, CHUNKS], BF16)
+        nc.vector.tensor_copy(out=chosen_columns[:], in_=ident[:, 0:CHUNKS])
+        gate_spread = gate_psum.tile([P, CHUNKS], F32, tag="gate")
+        nc.tensor.matmul(gate_spread[:], gate_bias_rows[:], chosen_columns[:], start=True, stop=True)
+        lin_spread = lin_psum.tile([P, D], F32, tag="lin")
+        nc.tensor.matmul(lin_spread[:], ones[:], lin_bias_row[:], start=True, stop=True)
         gate_bias = const.tile([P, CHUNKS], F32)
-
-        def transpose_gate_bias():
-            nc.vector.tensor_copy(out=gate_bias_rows_f32[:], in_=gate_bias_rows[:])
-            flipped = flip_psum.tile([P, P], F32, tag="flipped")
-            nc.tensor.transpose(flipped[:], gate_bias_rows_f32[:], ident[:])
-            nc.vector.tensor_copy(out=gate_bias[:], in_=flipped[:, 0:CHUNKS])
+        nc.vector.tensor_copy(out=gate_bias[:], in_=gate_spread[:])
+        lin_bias = const.tile([P, D], F32)
+        nc.vector.tensor_copy(out=lin_bias[:], in_=lin_spread[:])
 
         flipped_of = {}
         grouped_of = {}
@@ -159,7 +164,7 @@ def tile_smcmr_pb_t_kernel(
         def multiply_lin(tile_index):
             group, i = divmod(tile_index, GROUP_TILES)
             codes, planes = codes_of[group]
-            lin = lin_psum.tile([P, D], F32)
+            lin = lin_psum.tile([P, D], F32, tag="lin")
             for g in range(PASSES):
                 nc.tensor.matmul_mx(
                     out=lin[:],
@@ -185,7 +190,7 @@ def tile_smcmr_pb_t_kernel(
             group, part = divmod(step, STEPS_PER_GROUP)
             j = part * STEP_TILES + i
             codes, planes = codes_of[group]
-            gate = gate_psum.tile([P, GROUP_TOKENS], F32)
+            gate = gate_psum.tile([P, GROUP_TOKENS], F32, tag="gate")
             for g in range(PASSES):
                 nc.tensor.matmul_mx(
                     out=gate[:],
@@ -289,8 +294,5 @@ def tile_smcmr_pb_t_kernel(
             for tile_index in blend_tiles:
                 finish(tile_index)
 
-        for step in range(-FLIP_LEAD, 0):
-            one_round(step)
-        transpose_gate_bias()
-        for step in range(0, N_STEPS + BLEND_LAG):
+        for step in range(-FLIP_LEAD, N_STEPS + BLEND_LAG):
             one_round(step)

@@ -98,10 +98,11 @@ def tile_smcmr_pb_t_kernel(
         nc.sync.dma_start(out=gate_bias_rows[0:CHUNKS, :], in_=b_gate.rearrange("(j m) -> j m", m=P))
         nc.sync.dma_start(out=lin_bias_row[0:1, :], in_=b_lin.rearrange("(o d) -> o d", o=1))
         load_step(0)
-        load_weight(W_lin_words, lin_words, W_lin_scales, lin_planes)
         load_step(1)
+        load_weight(W_lin_words, lin_words, W_lin_scales, lin_planes)
+        load_step(2)
         load_weight(W_gate_words, gate_words, W_gate_scales, gate_planes)
-        for step in range(2, N_STEPS):
+        for step in range(3, N_STEPS):
             load_step(step)
 
         chosen_columns = const.tile([P, CHUNKS], BF16)

@@ -51,7 +51,7 @@ def tile_smcmr_pb_t_kernel(
         const = ctx.enter_context(tc.tile_pool(name="const", bufs=1))
         quant = ctx.enter_context(tc.tile_pool(name="quant", bufs=3))
         g_pool = ctx.enter_context(tc.tile_pool(name="g_pool", bufs=3))
-        h_pool = ctx.enter_context(tc.tile_pool(name="h_pool", bufs=STEP_TILES * (BLEND_LAG + 2)))
+        h_pool = ctx.enter_context(tc.tile_pool(name="h_pool", bufs=BLEND_LAG + 2))
         work = ctx.enter_context(tc.tile_pool(name="work", bufs=4 * STEP_TILES))
         results = ctx.enter_context(tc.tile_pool(name="results", bufs=3))
         flip_psum = ctx.enter_context(tc.psum_pool(name="flip_psum", bufs=STEP_TILES))
@@ -95,9 +95,9 @@ def tile_smcmr_pb_t_kernel(
                     in_=scales_dram[:, rows, :].rearrange("g r n -> r g n").bitcast(I32),
                 )
 
+        load_step(0)
         nc.sync.dma_start(out=gate_bias_rows[0:CHUNKS, :], in_=b_gate.rearrange("(j m) -> j m", m=P))
         nc.sync.dma_start(out=lin_bias_row[0:1, :], in_=b_lin.rearrange("(o d) -> o d", o=1))
-        load_step(0)
         load_step(1)
         load_weight(W_lin_words, lin_words, W_lin_scales, lin_planes)
         load_step(2)
@@ -108,13 +108,17 @@ def tile_smcmr_pb_t_kernel(
         chosen_columns = const.tile([P, CHUNKS], BF16)
         nc.vector.tensor_copy(out=chosen_columns[:], in_=ident[:, 0:CHUNKS])
         gate_spread = gate_psum.tile([P, CHUNKS], F32, tag="gate")
-        nc.tensor.matmul(gate_spread[:], gate_bias_rows[:], chosen_columns[:], start=True, stop=True)
-        lin_spread = lin_psum.tile([P, D], F32, tag="lin")
-        nc.tensor.matmul(lin_spread[:], ones[:], lin_bias_row[:], start=True, stop=True)
+        lin_spread = back_psum.tile([P, D], F32, tag="back")
         gate_bias = const.tile([P, CHUNKS], F32)
-        nc.vector.tensor_copy(out=gate_bias[:], in_=gate_spread[:])
         lin_bias = const.tile([P, D], F32)
-        nc.vector.tensor_copy(out=lin_bias[:], in_=lin_spread[:])
+
+        def spread_biases():
+            nc.tensor.matmul(gate_spread[:], gate_bias_rows[:], chosen_columns[:], start=True, stop=True)
+            nc.tensor.matmul(lin_spread[:], ones[:], lin_bias_row[:], start=True, stop=True)
+
+        def copy_biases():
+            nc.vector.tensor_copy(out=gate_bias[:], in_=gate_spread[:])
+            nc.scalar.copy(out=lin_bias[:], in_=lin_spread[:])
 
         flipped_of = {}
         grouped_of = {}
@@ -165,7 +169,7 @@ def tile_smcmr_pb_t_kernel(
         def multiply_lin(tile_index):
             group, i = divmod(tile_index, GROUP_TILES)
             codes, planes = codes_of[group]
-            lin = lin_psum.tile([P, D], F32, tag="lin")
+            lin = lin_psum.tile([P, D], F32)
             for g in range(PASSES):
                 nc.tensor.matmul_mx(
                     out=lin[:],
@@ -179,12 +183,14 @@ def tile_smcmr_pb_t_kernel(
             lin_of[tile_index] = lin
 
         def add_lin_bias(tile_index):
-            h = h_pool.tile([P, D], F32)
-            nc.vector.tensor_tensor(out=h[:], in0=lin_of[tile_index][:], in1=lin_bias[:], op=ALU.add)
-            h_of[tile_index] = h
+            step, i = divmod(tile_index, STEP_TILES)
+            if i == 0:
+                h = h_pool.tile([P, STEP_TILES, D], F32)
+                h_of[step] = h
+            nc.vector.tensor_tensor(out=h_of[step][:, i, :], in0=lin_of[tile_index][:], in1=lin_bias[:], op=ALU.add)
 
-        def tanh(tile_index):
-            h = h_of[tile_index]
+        def tanh(step):
+            h = h_of[step]
             nc.scalar.activation(out=h[:], in_=h[:], func=ACT.Tanh)
 
         def multiply_gate(step, i):
@@ -220,7 +226,7 @@ def tile_smcmr_pb_t_kernel(
 
         def transpose_g(tile_index):
             group, i = divmod(tile_index, GROUP_TILES)
-            back = back_psum.tile([P, D], F32)
+            back = back_psum.tile([P, D], F32, tag="back")
             for j in range(CHUNKS):
                 nc.tensor.transpose(
                     back[:, j * P : (j + 1) * P], g_t_of[group][:, j, i * P : (i + 1) * P], ident[:]
@@ -228,6 +234,7 @@ def tile_smcmr_pb_t_kernel(
             back_of[tile_index] = back
 
         def blend(tile_index):
+            step, i = divmod(tile_index, STEP_TILES)
             query_g = work.tile([P, D], F32)
             nc.vector.tensor_tensor(
                 out=query_g[:], in0=q_all[:, tile_index, :], in1=back_of[tile_index][:], op=ALU.mult
@@ -237,7 +244,7 @@ def tile_smcmr_pb_t_kernel(
                 out=rest[:],
                 in0=back_of[tile_index][:],
                 scalar=1.0,
-                in1=h_of[tile_index][:],
+                in1=h_of[step][:, i, :],
                 op0=ALU.subtract,
                 op1=ALU.mult,
             )
@@ -282,12 +289,15 @@ def tile_smcmr_pb_t_kernel(
                 quantise_cat(step + QUANT_LEAD)
             for tile_index in blend_tiles[1:]:
                 blend(tile_index)
+            if step == 0:
+                spread_biases()
+                copy_biases()
             for tile_index in lin_tiles:
                 add_lin_bias(tile_index)
             for part in gate_parts:
                 sigmoid(*part)
-            for tile_index in tiles_of(step - TANH_LAG):
-                tanh(tile_index)
+            if exists(step - TANH_LAG):
+                tanh(step - TANH_LAG)
             for tile_index in tiles_of(step + FLIP_LEAD):
                 transpose_cat(tile_index)
             for tile_index in tiles_of(step - BACK_LAG):

from contextlib import ExitStack

import concourse.mybir as mybir
from concourse.masks import make_identity

F32 = mybir.dt.float32
BF16 = mybir.dt.bfloat16
I32 = mybir.dt.int32
U32 = mybir.dt.uint32
U8 = mybir.dt.uint8
FP8X4 = mybir.dt.float8_e4m3fn_x4
FP4X4 = mybir.dt.float4_e2m1fn_x4
ALU = mybir.AluOpType
ACT = mybir.ActivationFunctionType

P = 128
PACK = 4
PAIR = 2
TOKENS = 16 * 256
D = 512
PASSES = 2
N_TILES = TOKENS // P
CHUNKS = D // P
GROUP_TILES = 4
GROUP_TOKENS = GROUP_TILES * P
STEP_TILES = 2
STEP_TOKENS = STEP_TILES * P
STEPS_PER_GROUP = GROUP_TILES // STEP_TILES
N_STEPS = N_TILES // STEP_TILES
FLIP_LEAD = 2
QUANT_LEAD = 1
GATE_LAG = 1
TANH_LAG = 1
BACK_LAG = 2
BLEND_LAG = 3
SCALE_ROWS = 4

FLOPS = 2 * TOKENS * (PASSES * D) * (2 * D)


def tile_smcmr_pb_t_kernel(
    tc, query, weighted_ctx, W_lin_words, W_lin_scales, b_lin, W_gate_words, W_gate_scales, b_gate, out
):
    nc = tc.nc
    q_dram = query.flatten_outer_dims().rearrange("(p t) d -> p t d", t=N_TILES)
    c_dram = weighted_ctx.flatten_outer_dims().rearrange("(p t) d -> p t d", t=N_TILES)
    out_dram = out.flatten_outer_dims().rearrange("(p t) d -> p t d", t=N_TILES)

    with ExitStack() as ctx:
        ctx.enter_context(tc.manual_schedule())
        const = ctx.enter_context(tc.tile_pool(name="const", bufs=1))
        quant = ctx.enter_context(tc.tile_pool(name="quant", bufs=3))
        g_pool = ctx.enter_context(tc.tile_pool(name="g_pool", bufs=3))
        h_pool = ctx.enter_context(tc.tile_pool(name="h_pool", bufs=BLEND_LAG + 2))
        work = ctx.enter_context(tc.tile_pool(name="work", bufs=4 * STEP_TILES))
        results = ctx.enter_context(tc.tile_pool(name="results", bufs=3))
        flip_psum = ctx.enter_context(tc.psum_pool(name="flip_psum", bufs=STEP_TILES))
        lin_psum = ctx.enter_context(tc.psum_pool(name="lin_psum", bufs=STEP_TILES))
        gate_psum = ctx.enter_context(tc.psum_pool(name="gate_psum", bufs=STEP_TILES))
        back_psum = ctx.enter_context(tc.psum_pool(name="back_psum", bufs=STEP_TILES))

        warm = const.tile([P, 1], F32)
        nc.vector.memset(warm[:], 0.0)
        nc.scalar.activation(out=warm[:], in_=warm[:], func=ACT.Sigmoid)

        lin_words = const.tile([P, PASSES, 2 * D], U8, align_bytes=64)
        lin_planes = const.tile([P, PASSES, D], U8, align_bytes=64)
        gate_words = const.tile([P, PASSES, 2 * D], U8, align_bytes=64)
        gate_planes = const.tile([P, PASSES, D], U8, align_bytes=64)
        gate_bias_rows = const.tile([P, P], BF16)
        nc.vector.memset(gate_bias_rows[:], 0.0)
        lin_bias_row = const.tile([P, D], BF16)
        nc.vector.memset(lin_bias_row[:], 0.0)
        ones = const.tile([P, P], BF16)
        nc.vector.memset(ones[:], 1.0)
        nc.vector.memset(lin_planes[:].bitcast(I32), 0)
        nc.vector.memset(gate_planes[:].bitcast(I32), 0)
        ident = const.tile([P, P], F32)
        make_identity(nc, ident[:])

        q_all = const.tile([P, N_TILES, D], BF16)
        c_all = const.tile([P, N_TILES, D], BF16)

        def load_step(step):
            tiles = slice(step * STEP_TILES, (step + 1) * STEP_TILES)
            nc.sync.dma_start(out=q_all[:, tiles, :], in_=q_dram[:, tiles, :])
            nc.sync.dma_start(out=c_all[:, tiles, :], in_=c_dram[:, tiles, :])

        def load_weight(words_dram, words, scales_dram, planes):
            nc.sync.dma_start(out=words[:].bitcast(I32), in_=words_dram.rearrange("g p b -> p g b").bitcast(I32))
            for quadrant in range(P // 32):
                rows = slice(SCALE_ROWS * quadrant, SCALE_ROWS * (quadrant + 1))
                nc.sync.dma_start(
                    out=planes[32 * quadrant : 32 * quadrant + SCALE_ROWS, :, :].bitcast(I32),
                    in_=scales_dram[:, rows, :].rearrange("g r n -> r g n").bitcast(I32),
                )

        load_step(0)
        nc.sync.dma_start(out=gate_bias_rows[0:CHUNKS, :], in_=b_gate.rearrange("(j m) -> j m", m=P))
        nc.sync.dma_start(out=lin_bias_row[0:1, :], in_=b_lin.rearrange("(o d) -> o d", o=1))
        load_step(1)
        load_weight(W_lin_words, lin_words, W_lin_scales, lin_planes)
        load_step(2)
        load_weight(W_gate_words, gate_words, W_gate_scales, gate_planes)
        for step in range(3, N_STEPS):
            load_step(step)

        chosen_columns = const.tile([P, CHUNKS], BF16)
        nc.vector.tensor_copy(out=chosen_columns[:], in_=ident[:, 0:CHUNKS])
        gate_spread = gate_psum.tile([P, CHUNKS], F32, tag="gate")
        lin_spread = back_psum.tile([P, D], F32, tag="back")
        gate_bias = const.tile([P, CHUNKS], F32)
        lin_bias = const.tile([P, D], F32)

        def spread_biases():
            nc.tensor.matmul(gate_spread[:], gate_bias_rows[:], chosen_columns[:], start=True, stop=True)
            nc.tensor.matmul(lin_spread[:], ones[:], lin_bias_row[:], start=True, stop=True)

        def copy_biases():
            nc.vector.tensor_copy(out=gate_bias[:], in_=gate_spread[:])
            nc.scalar.copy(out=lin_bias[:], in_=lin_spread[:])

        flipped_of = {}
        grouped_of = {}
        codes_of = {}
        lin_of = {}
        h_of = {}
        gate_of = {}
        g_t_of = {}
        back_of = {}
        query_g_of = {}
        rest_of = {}
        result_of = {}

        def transpose_cat(tile_index):
            flipped = flip_psum.tile([P, PASSES, PAIR, P], F32, tag="flipped")
            for g, resident in enumerate((q_all, c_all)):
                words = resident[:, tile_index, :].bitcast(F32)
                for u in range(PAIR):
                    nc.tensor.transpose(flipped[:, g, u, :], words[:, u : D // PAIR : PAIR], ident[:])
            flipped_of[tile_index] = flipped

        def copy_cat(tile_index, copy):
            step, i = divmod(tile_index, STEP_TILES)
            if i == 0:
                grouped = quant.tile([P, PASSES, STEP_TOKENS, PACK], BF16, align_bytes=64)
                grouped_of[step] = grouped
            grouped_words = grouped_of[step][:].bitcast(F32)
            copy(
                out=grouped_words[:, :, i * P : (i + 1) * P, :],
                in_=flipped_of[tile_index][:].rearrange("p g u r -> p g r u"),
            )

        def quantise_cat(step):
            group, part = divmod(step, STEPS_PER_GROUP)
            if part == 0:
                codes = quant.tile([P, PASSES, GROUP_TOKENS], U32, align_bytes=64)
                planes = quant.tile([P, PASSES, GROUP_TOKENS], U8, align_bytes=64)
                codes_of[group] = (codes, planes)
            codes, planes = codes_of[group]
            tokens = slice(part * STEP_TOKENS, (part + 1) * STEP_TOKENS)
            for g in range(PASSES):
                nc.vector.quantize_mx(
                    out=codes[:, g, tokens].bitcast(FP8X4),
                    scales=planes[:, g, tokens],
                    in_=grouped_of[step][:, g, :, :].rearrange("p r t -> p (r t)"),
                )

        def multiply_lin(tile_index):
            group, i = divmod(tile_index, GROUP_TILES)
            codes, planes = codes_of[group]
            lin = lin_psum.tile([P, D], F32)
            for g in range(PASSES):
                nc.tensor.matmul_mx(
                    out=lin[:],
                    lhsT=codes[:, g, i * P : (i + 1) * P].bitcast(FP8X4),
                    lhsT_scale=planes[:, g, i * P : (i + 1) * P],
                    rhs=lin_words[:, g, :].bitcast(FP4X4),
                    rhs_scale=lin_planes[:, g, :],
                    start=(g == 0),
                    stop=(g == PASSES - 1),
                )
            lin_of[tile_index] = lin

        def add_lin_bias(tile_index):
            step, i = divmod(tile_index, STEP_TILES)
            if i == 0:
                h = h_pool.tile([P, STEP_TILES, D], F32)
                h_of[step] = h
            nc.vector.tensor_tensor(out=h_of[step][:, i, :], in0=lin_of[tile_index][:], in1=lin_bias[:], op=ALU.add)

        def tanh(step):
            h = h_of[step]
            nc.scalar.activation(out=h[:], in_=h[:], func=ACT.Tanh)

        def multiply_gate(step, i):
            group, part = divmod(step, STEPS_PER_GROUP)
            j = part * STEP_TILES + i
            codes, planes = codes_of[group]
            gate = gate_psum.tile([P, GROUP_TOKENS], F32, tag="gate")
            for g in range(PASSES):
                nc.tensor.matmul_mx(
                    out=gate[:],
                    lhsT=gate_words[:, g, 2 * j * P : 2 * (j + 1) * P].bitcast(FP4X4),
                    lhsT_scale=gate_planes[:, g, j * P : (j + 1) * P],
                    rhs=codes[:, g, :].bitcast(FP8X4),
                    rhs_scale=planes[:, g, :],
                    start=(g == 0),
                    stop=(g == PASSES - 1),
                )
            gate_of[step, i] = gate

        def sigmoid(step, i):
            group, part = divmod(step, STEPS_PER_GROUP)
            j = part * STEP_TILES + i
            if j == 0:
                g_t = g_pool.tile([P, CHUNKS, GROUP_TOKENS], F32)
                g_t_of[group] = g_t
            nc.scalar.activation(
                out=g_t_of[group][:, j, :],
                in_=gate_of[step, i][:],
                func=ACT.Sigmoid,
                bias=gate_bias[:, j : j + 1],
                scale=1.0,
            )

        def transpose_g(tile_index):
            group, i = divmod(tile_index, GROUP_TILES)
            back = back_psum.tile([P, D], F32, tag="back")
            for j in range(CHUNKS):
                nc.tensor.transpose(
                    back[:, j * P : (j + 1) * P], g_t_of[group][:, j, i * P : (i + 1) * P], ident[:]
                )
            back_of[tile_index] = back

        def blend(tile_index):
            step, i = divmod(tile_index, STEP_TILES)
            query_g = work.tile([P, D], F32)
            nc.vector.tensor_tensor(
                out=query_g[:], in0=q_all[:, tile_index, :], in1=back_of[tile_index][:], op=ALU.mult
            )
            rest = work.tile([P, D], F32)
            nc.vector.scalar_tensor_tensor(
                out=rest[:],
                in0=back_of[tile_index][:],
                scalar=1.0,
                in1=h_of[step][:, i, :],
                op0=ALU.subtract,
                op1=ALU.mult,
            )
            query_g_of[tile_index] = query_g
            rest_of[tile_index] = rest

        def finish(tile_index):
            step, i = divmod(tile_index, STEP_TILES)
            if i == 0:
                result = results.tile([P, STEP_TILES, D], F32)
                result_of[step] = result
            result = result_of[step]
            engine = nc.vector if tile_index == N_TILES - 1 else nc.gpsimd
            engine.tensor_tensor(
                out=result[:, i, :], in0=query_g_of[tile_index][:], in1=rest_of[tile_index][:], op=ALU.subtract
            )
            if step == N_STEPS - 1:
                nc.sync.dma_start(out=out_dram[:, tile_index, :], in_=result[:, i, :])
            elif i == STEP_TILES - 1:
                tiles = slice(step * STEP_TILES, (step + 1) * STEP_TILES)
                nc.sync.dma_start(out=out_dram[:, tiles, :], in_=result[:])

        def tiles_of(step):
            return range(step * STEP_TILES, (step + 1) * STEP_TILES) if 0 <= step < N_STEPS else ()

        def exists(step):
            return 0 <= step < N_STEPS

        def one_round(step):
            gate_parts = [(step - GATE_LAG, i) for i in range(STEP_TILES)] if exists(step - GATE_LAG) else []
            lin_tiles = tiles_of(step)
            blend_tiles = tiles_of(step - BLEND_LAG)
            for part in gate_parts:
                multiply_gate(*part)
            for tile_index in lin_tiles:
                multiply_lin(tile_index)
            for tile_index in tiles_of(step + QUANT_LEAD):
                copy_cat(tile_index, nc.vector.tensor_copy if tile_index == 1 else nc.scalar.copy)
            for tile_index in blend_tiles[:1]:
                blend(tile_index)
            if exists(step + QUANT_LEAD):
                quantise_cat(step + QUANT_LEAD)
            for tile_index in blend_tiles[1:]:
                blend(tile_index)
            if step == 0:
                spread_biases()
                copy_biases()
            for tile_index in lin_tiles:
                add_lin_bias(tile_index)
            for part in gate_parts:
                sigmoid(*part)
            if exists(step - TANH_LAG):
                tanh(step - TANH_LAG)
            for tile_index in tiles_of(step + FLIP_LEAD):
                transpose_cat(tile_index)
            for tile_index in tiles_of(step - BACK_LAG):
                transpose_g(tile_index)
            for tile_index in blend_tiles:
                finish(tile_index)

        for step in range(-FLIP_LEAD, N_STEPS + BLEND_LAG):
            one_round(step)
